import numpy as np
import ml_dtypes


BF16 = ml_dtypes.bfloat16


def bf(x):
    return np.asarray(x, np.float32).astype(BF16)


def f64(x):
    return np.asarray(x).astype(np.float64)


E2M1 = np.array([0.0, 0.5, 1.0, 1.5, 2.0, 3.0, 4.0, 6.0, -0.0, -0.5, -1.0, -1.5, -2.0, -3.0, -4.0, -6.0])


def pack_weight(w, fmt):
    k, n = w.shape
    w = f64(bf(w)).reshape(k // 32, 32, n)
    amax = np.abs(w).max(1)
    if fmt == "e4m3":
        byte = np.frexp(amax)[1] - 1 + 127 - 7
    else:
        mant, ex = np.frexp(amax / 6.0)
        byte = np.where(mant > 0.5, ex, ex - 1) + 127
    byte = np.clip(np.where(amax > 0, byte, 1), 1, 254)
    scaled = (w * np.exp2(127.0 - byte)[:, None, :]).reshape(k, n).astype(np.float32)
    by_word = np.ascontiguousarray(scaled.reshape(k // 512, 128, 4, n).transpose(0, 1, 3, 2))
    if fmt == "e4m3":
        words = by_word.astype(ml_dtypes.float8_e4m3fn).view(np.uint8)
    else:
        c = by_word.astype(ml_dtypes.float4_e2m1fn).view(np.uint8) & 0xF
        words = c[..., 0::2] | (c[..., 1::2] << 4)
    return np.ascontiguousarray(words), np.ascontiguousarray(byte.astype(np.uint8).reshape(k // 512, 16, n))


def unpack_weight(words, scales, fmt):
    g, p, n, _ = words.shape
    if fmt == "e4m3":
        vals = np.ascontiguousarray(words).view(ml_dtypes.float8_e4m3fn).astype(np.float64)
    else:
        nib = np.empty((g, p, n, 4), np.uint8)
        nib[..., 0::2] = words & 0xF
        nib[..., 1::2] = words >> 4
        vals = E2M1[nib]
    vals = vals * np.repeat(np.exp2(scales.astype(np.float64) - 127.0), 8, axis=1)[..., None]
    return vals.transpose(0, 1, 3, 2).reshape(g * 512, n)

def pack4(w):
    words, scales = pack_weight(w, "e2m1")
    return words.reshape(words.shape[0], 128, -1), scales


def unpack4(words, scales):
    return unpack_weight(words.reshape(words.shape[0], 128, -1, 2), scales, "e2m1")


def kspread(k):
    return np.exp2(np.repeat(np.random.randint(-6, 7, k // 32), 32).astype(np.float64))


B, S, HID, NH, HD, RD, RATIO = 1, 1536, 3072, 8, 128, 64, 4
THETA = 10000.0
HALF = RD // 2


def rope_tables(positions):
    inv_freq = 1.0 / THETA ** (np.arange(HALF) / HALF)
    ang = positions[:, None] * inv_freq[None, :]
    return np.cos(ang), np.sin(ang)


def rope_interleaved(x, cos, sin):
    nope, rope = x[..., :-RD], x[..., -RD:]
    pr = rope.reshape(rope.shape[:-1] + (HALF, 2))
    a, b = pr[..., 0], pr[..., 1]
    new = np.stack([a * cos - b * sin, a * sin + b * cos], axis=-1).reshape(rope.shape)
    return np.concatenate([nope, new], axis=-1)


def setup_inputs():
    s = kspread(HID)
    hidden = np.random.standard_normal((B, S, HID)) * s
    hidden_words, hidden_scales = pack4(hidden.reshape(B * S, HID).T)
    wq_words, wq_scales = pack4(np.random.standard_normal((HID, NH * HD)) / np.sqrt(HID) / s[:, None])
    return {"hidden_words": hidden_words,
            "hidden_scales": hidden_scales,
            "wq_words": wq_words,
            "wq_scales": wq_scales}


def reference(hidden_words, hidden_scales, wq_words, wq_scales):
    q = unpack4(hidden_words, hidden_scales).T.reshape(B, S, HID) @ unpack4(wq_words, wq_scales)
    q = q.reshape(B, S, NH, HD).transpose(0, 2, 1, 3)
    cq, sq = rope_tables(np.arange(S))
    return rope_interleaved(q, cq, sq)

@@ -1,0 +1,158 @@
+import math
+from contextlib import ExitStack
+
+import concourse.mybir as mybir
+
+FLOPS = 2 * 1536 * 1024 * 3072
+
+F32 = mybir.dt.float32
+BF16 = mybir.dt.bfloat16
+I32 = mybir.dt.int32
+U8 = mybir.dt.uint8
+FP4X4 = mybir.dt.float4_e2m1fn_x4
+ALU = mybir.AluOpType
+
+P = 128
+PASSES = 6
+TOKENS = 1536
+CHUNK = 512
+T_TILES = TOKENS // P
+HD = 128
+ROPE = 64
+HALF = ROPE // 2
+N_BLOCK = 512
+WARM = 8
+QUADS = (0, 2, 1, 3)
+
+
+def tile_deepseekv4attention_pb_kernel(tc, hidden_words, hidden_scales, wq_words, wq_scales, out):
+    nc = tc.nc
+    with ExitStack() as ctx:
+        keep = ctx.enter_context(tc.tile_pool(name="keep", bufs=1))
+        work = ctx.enter_context(tc.tile_pool(name="work", bufs=6))
+        psum = ctx.enter_context(tc.psum_pool(name="psum", bufs=8))
+        ctx.enter_context(tc.manual_schedule())
+
+        def load(tile_ap, dram_ap):
+            nc.sync.dma_start(out=tile_ap.bitcast(I32), in_=dram_ap.bitcast(I32))
+
+        def load_scales(planes, scales, g0, g1, c0, c1):
+            for q in QUADS:
+                load(planes[32 * q : 32 * q + 4, :, :],
+                     scales[g0:g1, 4 * q : 4 * q + 4, c0:c1].rearrange("g r n -> r g n"))
+
+        warm = keep.tile([P, 640], BF16, name="warm")
+        pos = keep.tile([P, T_TILES], F32, name="pos")
+        xs_a = keep.tile([P, PASSES, CHUNK], U8, name="xs_a", align_bytes=256)
+        ws_a = keep.tile([P, 3, 1024], U8, name="ws_a", align_bytes=256)
+        ws_b = keep.tile([P, 3, 1024], U8, name="ws_b", align_bytes=256)
+        xs_b = keep.tile([P, PASSES, 2 * CHUNK], U8, name="xs_b", align_bytes=256)
+        x_a = [keep.tile([P, 2 * CHUNK], U8, name="x_a%d" % g, align_bytes=256) for g in range(PASSES)]
+        w_0 = [keep.tile([P, 2 * N_BLOCK], U8, name="w_0%d" % b, align_bytes=256) for b in range(2)]
+        w_r = [keep.tile([P, 4 * N_BLOCK], U8, name="w_r%d" % g, align_bytes=256) for g in range(1, PASSES)]
+        x_b = keep.tile([P, PASSES, 2 * CHUNK], U8, name="x_b", align_bytes=256)
+        x_c = keep.tile([P, PASSES, 2 * CHUNK], U8, name="x_c", align_bytes=256)
+
+        nc.gpsimd.memset(warm[:], 0.0)
+        nc.gpsimd.iota(pos[:], [[P, T_TILES]], base=0, channel_multiplier=1, allow_small_or_imprecise_dtypes=True)
+        for planes in (xs_a, ws_a, ws_b, xs_b):
+            nc.vector.memset(planes[:].bitcast(I32), 0)
+
+        load(x_a[0][:], hidden_words[0, :, 0 : 2 * CHUNK])
+        load(w_0[0][:], wq_words[0, :, 0 : 2 * N_BLOCK])
+        load_scales(xs_a, hidden_scales, 0, PASSES, 0, CHUNK)
+        load_scales(ws_a, wq_scales, 0, 3, 0, 1024)
+        load(w_0[1][:], wq_words[0, :, 2 * N_BLOCK : 4 * N_BLOCK])
+        for g in range(1, PASSES):
+            load(x_a[g][:], hidden_words[g, :, 0 : 2 * CHUNK])
+            load(w_r[g - 1][:], wq_words[g, :, :])
+            if g == 2:
+                load_scales(ws_b, wq_scales, 3, PASSES, 0, 1024)
+        load_scales(xs_b, hidden_scales, 0, PASSES, CHUNK, 3 * CHUNK)
+        load(x_b[:], hidden_words[:, :, 2 * CHUNK : 4 * CHUNK].rearrange("g p c -> p g c"))
+        load(x_c[:], hidden_words[:, :, 4 * CHUNK : 6 * CHUNK].rearrange("g p c -> p g c"))
+
+        ang = keep.tile([P, T_TILES, 2, ROPE], F32, name="ang")
+        whole = keep.tile([P, T_TILES * 2 * ROPE], I32, name="whole")
+        table = keep.tile([P, T_TILES, 2, ROPE], F32, name="table")
+        turn = 1.0 / (2.0 * math.pi)
+        pos3 = pos[:].unsqueeze(2)
+        for kind, e, factor in ((0, 0, turn), (0, 1, turn), (1, 0, turn), (1, 1, -turn)):
+            nc.vector.tensor_scalar(out=ang[:, :, kind, e : e + 1], in0=pos3, scalar1=factor, scalar2=None, op0=ALU.mult)
+        rows = ang[:].rearrange("p t k c -> p (t k) c")
+        s = 1
+        while s < HALF:
+            nc.vector.tensor_scalar(out=rows[:, :, 2 * s : 4 * s], in0=rows[:, :, 0 : 2 * s],
+                                    scalar1=10000.0 ** (-s / HALF), scalar2=None, op0=ALU.mult)
+            s *= 2
+        nc.vector.tensor_scalar(out=ang[:, :, 0, :], in0=ang[:, :, 0, :], scalar1=0.25, scalar2=None, op0=ALU.add)
+        flat = ang[:].rearrange("p t k c -> p (t k c)")
+        nc.vector.tensor_copy(out=whole[:], in_=flat)
+        nc.vector.tensor_tensor(out=flat, in0=flat, in1=whole[:], op=ALU.subtract)
+        nc.scalar.activation(out=table[:].rearrange("p t k c -> p (t k c)"), in_=flat,
+                             func=mybir.ActivationFunctionType.Sin, scale=2.0 * math.pi)
+
+        def x_operand(g, t):
+            if t < 4:
+                return x_a[g][:, 256 * t : 256 * (t + 1)], xs_a[:, g, P * t : P * (t + 1)]
+            codes = x_b if t < 8 else x_c
+            c = 256 * (t % 4)
+            return codes[:, g, c : c + 256], xs_b[:, g, P * (t - 4) : P * (t - 3)]
+
+        def w_operand(g, h0, nh):
+            c0, c1 = HD * h0, HD * (h0 + nh)
+            planes = ws_a if g < 3 else ws_b
+            if g == 0:
+                b = h0 // 4
+                codes = w_0[b][:, 2 * (c0 - N_BLOCK * b) : 2 * (c1 - N_BLOCK * b)]
+            else:
+                codes = w_r[g - 1][:, 2 * c0 : 2 * c1]
+            return codes, planes[:, g % 3, c0:c1]
+
+        def one_pass(acc, g, t, h0, nh):
+            xc, xs = x_operand(g, t)
+            wc, ws = w_operand(g, h0, nh)
+            nc.tensor.matmul_mx(out=acc[:, 0 : HD * nh], lhsT=xc.bitcast(FP4X4), lhsT_scale=xs,
+                                rhs=wc.bitcast(FP4X4), rhs_scale=ws, start=(g == 0), stop=(g == PASSES - 1))
+
+        def multiply(acc, t, nh):
+            y = acc[:, 0 : HD * nh].rearrange("p (h d) -> p h d", d=HD)
+            prod = work.tile([P, 2, nh, ROPE], F32, name="prod")
+            shape = [P, 2, nh, ROPE]
+            nc.vector.tensor_tensor(out=prod[:], in0=y[:, :, HD - ROPE : HD].unsqueeze(1).to_broadcast(shape),
+                                    in1=table[:, t, :, :].unsqueeze(2).to_broadcast(shape), op=ALU.mult)
+            res = work.tile([P, nh, HD], F32, name="res")
+            nc.scalar.copy(out=res[:, :, 0 : HD - ROPE], in_=y[:, :, 0 : HD - ROPE])
+            return prod, res
+
+        def add_and_store(prod, res, t, h0, nh):
+            pair = "p h (j e) -> p h j e"
+            nc.vector.tensor_tensor(out=res[:, :, HD - ROPE : HD].rearrange(pair, e=2),
+                                    in0=prod[:, 0, :, :].rearrange(pair, e=2),
+                                    in1=prod[:, 1, :, :].rearrange(pair, e=2)[:, :, :, ::-1], op=ALU.add)
+            nc.sync.dma_start(out=out[0, h0 : h0 + nh, P * t : P * (t + 1), :].rearrange("h p d -> p h d"), in_=res[:])
+
+        scrap = psum.tile([P, N_BLOCK], F32, name="acc")
+        for k in range(WARM):
+            nc.tensor.matmul(out=scrap[:], lhsT=warm[:, 0:P], rhs=warm[:, P : P + N_BLOCK], start=True, stop=True)
+
+        first = [(t, 4 * b, psum.tile([P, N_BLOCK], F32, name="acc")) for b in range(2) for t in range(4)]
+        for g in range(PASSES):
+            for t, h0, acc in first:
+                one_pass(acc, g, t, h0, 4)
+        waiting = []
+        for t, h0, acc in first:
+            waiting.append((multiply(acc, t, 4), t, h0))
+            if len(waiting) == 2:
+                (prod, res), tw, hw = waiting.pop(0)
+                add_and_store(prod, res, tw, hw, 4)
+        (prod, res), tw, hw = waiting.pop(0)
+        add_and_store(prod, res, tw, hw, 4)
+
+        for t in range(4, T_TILES):
+            for h0, nh in ((0, 4), (4, 4)) if t < T_TILES - 1 else ((0, 4), (4, 2), (6, 1), (7, 1)):
+                acc = psum.tile([P, N_BLOCK], F32, name="acc")
+                for g in range(PASSES):
+                    one_pass(acc, g, t, h0, nh)
+                prod, res = multiply(acc, t, nh)
+                add_and_store(prod, res, t, h0, nh)

@@ -21,7 +21,7 @@ HD = 128
 ROPE = 64
 HALF = ROPE // 2
 N_BLOCK = 512
-WARM = 8
+WARM = 7
 QUADS = (0, 2, 1, 3)
 
 
@@ -117,12 +117,15 @@ def tile_deepseekv4attention_pb_kernel(tc, hidden_words, hidden_scales, wq_words
 
         def multiply(acc, t, nh):
             y = acc[:, 0 : HD * nh].rearrange("p (h d) -> p h d", d=HD)
+            res = work.tile([P, nh, HD], F32, name="res")
+            if nh > 2:
+                nc.scalar.copy(out=res[:, :, 0 : HD - ROPE], in_=y[:, :, 0 : HD - ROPE])
             prod = work.tile([P, 2, nh, ROPE], F32, name="prod")
             shape = [P, 2, nh, ROPE]
             nc.vector.tensor_tensor(out=prod[:], in0=y[:, :, HD - ROPE : HD].unsqueeze(1).to_broadcast(shape),
                                     in1=table[:, t, :, :].unsqueeze(2).to_broadcast(shape), op=ALU.mult)
-            res = work.tile([P, nh, HD], F32, name="res")
-            nc.scalar.copy(out=res[:, :, 0 : HD - ROPE], in_=y[:, :, 0 : HD - ROPE])
+            if nh <= 2:
+                nc.scalar.copy(out=res[:, :, 0 : HD - ROPE], in_=y[:, :, 0 : HD - ROPE])
             return prod, res
 
         def add_and_store(prod, res, t, h0, nh):
@@ -140,19 +143,26 @@ def tile_deepseekv4attention_pb_kernel(tc, hidden_words, hidden_scales, wq_words
         for g in range(PASSES):
             for t, h0, acc in first:
                 one_pass(acc, g, t, h0, 4)
-        waiting = []
-        for t, h0, acc in first:
-            waiting.append((multiply(acc, t, 4), t, h0))
-            if len(waiting) == 2:
-                (prod, res), tw, hw = waiting.pop(0)
-                add_and_store(prod, res, tw, hw, 4)
-        (prod, res), tw, hw = waiting.pop(0)
-        add_and_store(prod, res, tw, hw, 4)
+        def drain(groups):
+            held = None
+            for group in groups:
+                acc, t, h0, nh = group
+                parts = multiply(acc, t, nh)
+                if held is not None:
+                    add_and_store(*held)
+                held = (*parts, t, h0, nh)
+            add_and_store(*held)
 
-        for t in range(4, T_TILES):
-            for h0, nh in ((0, 4), (4, 4)) if t < T_TILES - 1 else ((0, 4), (4, 2), (6, 1), (7, 1)):
-                acc = psum.tile([P, N_BLOCK], F32, name="acc")
-                for g in range(PASSES):
-                    one_pass(acc, g, t, h0, nh)
-                prod, res = multiply(acc, t, nh)
-                add_and_store(prod, res, t, h0, nh)
+        def compute(t, h0, nh):
+            acc = psum.tile([P, N_BLOCK], F32, name="acc")
+            for g in range(PASSES):
+                one_pass(acc, g, t, h0, nh)
+            return acc, t, h0, nh
+
+        drain([(acc, t, h0, 4) for t, h0, acc in first])
+        for t in range(4, T_TILES - 1):
+            for h0 in (0, 4):
+                drain([compute(t, h0, 4)])
+        last = T_TILES - 1
+        drain([compute(last, 0, 4)])
+        drain([compute(last, 4, 2), compute(last, 6, 1), compute(last, 7, 1)])

@@ -23,6 +23,7 @@ HALF = ROPE // 2
 N_BLOCK = 512
 WARM = 7
 QUADS = (0, 2, 1, 3)
+W_CODES_AT, W_SCALES_AT, X_CODES_AT, X_SCALES_AT = 0, 64, 128, 192
 
 
 def tile_deepseekv4attention_pb_kernel(tc, hidden_words, hidden_scales, wq_words, wq_scales, out):
@@ -43,34 +44,44 @@ def tile_deepseekv4attention_pb_kernel(tc, hidden_words, hidden_scales, wq_words
 
         warm = keep.tile([P, 640], BF16, name="warm")
         pos = keep.tile([P, T_TILES], F32, name="pos")
-        xs_a = keep.tile([P, PASSES, CHUNK], U8, name="xs_a", align_bytes=256)
-        ws_a = keep.tile([P, 3, 1024], U8, name="ws_a", align_bytes=256)
-        ws_b = keep.tile([P, 3, 1024], U8, name="ws_b", align_bytes=256)
-        xs_b = keep.tile([P, PASSES, 2 * CHUNK], U8, name="xs_b", align_bytes=256)
-        x_a = [keep.tile([P, 2 * CHUNK], U8, name="x_a%d" % g, align_bytes=256) for g in range(PASSES)]
-        w_0 = [keep.tile([P, 2 * N_BLOCK], U8, name="w_0%d" % b, align_bytes=256) for b in range(2)]
-        w_r = [keep.tile([P, 4 * N_BLOCK], U8, name="w_r%d" % g, align_bytes=256) for g in range(1, PASSES)]
-        x_b = keep.tile([P, PASSES, 2 * CHUNK], U8, name="x_b", align_bytes=256)
-        x_c = keep.tile([P, PASSES, 2 * CHUNK], U8, name="x_c", align_bytes=256)
+        def placed(name, width, offset):
+            whole_tile = keep.tile([P, offset + width], U8, name=name, align_bytes=256)
+            return whole_tile[:, offset : offset + width]
+
+        def planes_at(name, passes, width, offset):
+            return placed(name, passes * width, offset).rearrange("p (g n) -> p g n", g=passes)
+
+        xs_a0 = planes_at("xs_a0", 2, CHUNK, X_SCALES_AT)
+        xs_a1 = planes_at("xs_a1", PASSES - 2, CHUNK, X_SCALES_AT)
+        xs_b = planes_at("xs_b", PASSES, 2 * CHUNK, X_SCALES_AT)
+        ws_a = planes_at("ws_a", 3, 1024, W_SCALES_AT)
+        ws_b = planes_at("ws_b", 3, 1024, W_SCALES_AT)
+        x_a = [placed("x_a%d" % g, 2 * CHUNK, X_CODES_AT) for g in range(PASSES)]
+        x_b = planes_at("x_b", PASSES, 2 * CHUNK, X_CODES_AT)
+        x_c = planes_at("x_c", PASSES, 2 * CHUNK, X_CODES_AT)
+        w_0 = [placed("w_0%d" % b, 2 * N_BLOCK, W_CODES_AT) for b in range(2)]
+        w_r = [placed("w_r%d" % g, 4 * N_BLOCK, W_CODES_AT) for g in range(1, PASSES)]
 
         nc.gpsimd.memset(warm[:], 0.0)
         nc.gpsimd.iota(pos[:], [[P, T_TILES]], base=0, channel_multiplier=1, allow_small_or_imprecise_dtypes=True)
-        for planes in (xs_a, ws_a, ws_b, xs_b):
-            nc.vector.memset(planes[:].bitcast(I32), 0)
+        for planes in (ws_a, xs_a0, xs_a1, ws_b, xs_b):
+            nc.vector.memset(planes.bitcast(I32), 0)
 
-        load(x_a[0][:], hidden_words[0, :, 0 : 2 * CHUNK])
-        load(w_0[0][:], wq_words[0, :, 0 : 2 * N_BLOCK])
-        load_scales(xs_a, hidden_scales, 0, PASSES, 0, CHUNK)
+        load(x_a[0], hidden_words[0, :, 0 : 2 * CHUNK])
+        load(w_0[0], wq_words[0, :, 0 : 2 * N_BLOCK])
         load_scales(ws_a, wq_scales, 0, 3, 0, 1024)
-        load(w_0[1][:], wq_words[0, :, 2 * N_BLOCK : 4 * N_BLOCK])
+        load_scales(xs_a0, hidden_scales, 0, 2, 0, CHUNK)
+        load(w_0[1], wq_words[0, :, 2 * N_BLOCK : 4 * N_BLOCK])
         for g in range(1, PASSES):
-            load(x_a[g][:], hidden_words[g, :, 0 : 2 * CHUNK])
-            load(w_r[g - 1][:], wq_words[g, :, :])
+            load(x_a[g], hidden_words[g, :, 0 : 2 * CHUNK])
+            load(w_r[g - 1], wq_words[g, :, :])
+            if g == 1:
+                load_scales(xs_a1, hidden_scales, 2, PASSES, 0, CHUNK)
             if g == 2:
                 load_scales(ws_b, wq_scales, 3, PASSES, 0, 1024)
         load_scales(xs_b, hidden_scales, 0, PASSES, CHUNK, 3 * CHUNK)
-        load(x_b[:], hidden_words[:, :, 2 * CHUNK : 4 * CHUNK].rearrange("g p c -> p g c"))
-        load(x_c[:], hidden_words[:, :, 4 * CHUNK : 6 * CHUNK].rearrange("g p c -> p g c"))
+        load(x_b, hidden_words[:, :, 2 * CHUNK : 4 * CHUNK].rearrange("g p c -> p g c"))
+        load(x_c, hidden_words[:, :, 4 * CHUNK : 6 * CHUNK].rearrange("g p c -> p g c"))
 
         ang = keep.tile([P, T_TILES, 2, ROPE], F32, name="ang")
         whole = keep.tile([P, T_TILES * 2 * ROPE], I32, name="whole")
@@ -94,7 +105,8 @@ def tile_deepseekv4attention_pb_kernel(tc, hidden_words, hidden_scales, wq_words
 
         def x_operand(g, t):
             if t < 4:
-                return x_a[g][:, 256 * t : 256 * (t + 1)], xs_a[:, g, P * t : P * (t + 1)]
+                scales = xs_a0[:, g] if g < 2 else xs_a1[:, g - 2]
+                return x_a[g][:, 256 * t : 256 * (t + 1)], scales[:, P * t : P * (t + 1)]
             codes = x_b if t < 8 else x_c
             c = 256 * (t % 4)
             return codes[:, g, c : c + 256], xs_b[:, g, P * (t - 4) : P * (t - 3)]
@@ -109,10 +121,10 @@ def tile_deepseekv4attention_pb_kernel(tc, hidden_words, hidden_scales, wq_words
                 codes = w_r[g - 1][:, 2 * c0 : 2 * c1]
             return codes, planes[:, g % 3, c0:c1]
 
-        def one_pass(acc, g, t, h0, nh):
+        def one_pass(acc, g, t, weights):
             xc, xs = x_operand(g, t)
-            wc, ws = w_operand(g, h0, nh)
-            nc.tensor.matmul_mx(out=acc[:, 0 : HD * nh], lhsT=xc.bitcast(FP4X4), lhsT_scale=xs,
+            wc, ws = weights
+            nc.tensor.matmul_mx(out=acc[:, 0 : ws.shape[1]], lhsT=xc.bitcast(FP4X4), lhsT_scale=xs,
                                 rhs=wc.bitcast(FP4X4), rhs_scale=ws, start=(g == 0), stop=(g == PASSES - 1))
 
         def multiply(acc, t, nh):
@@ -142,7 +154,7 @@ def tile_deepseekv4attention_pb_kernel(tc, hidden_words, hidden_scales, wq_words
         first = [(t, 4 * b, psum.tile([P, N_BLOCK], F32, name="acc")) for b in range(2) for t in range(4)]
         for g in range(PASSES):
             for t, h0, acc in first:
-                one_pass(acc, g, t, h0, 4)
+                one_pass(acc, g, t, w_operand(g, h0, 4))
         def drain(groups):
             held = None
             for group in groups:
@@ -156,7 +168,7 @@ def tile_deepseekv4attention_pb_kernel(tc, hidden_words, hidden_scales, wq_words
         def compute(t, h0, nh):
             acc = psum.tile([P, N_BLOCK], F32, name="acc")
             for g in range(PASSES):
-                one_pass(acc, g, t, h0, nh)
+                one_pass(acc, g, t, w_operand(g, h0, nh))
             return acc, t, h0, nh
 
         drain([(acc, t, h0, 4) for t, h0, acc in first])

@@ -21,8 +21,10 @@ HD = 128
 ROPE = 64
 HALF = ROPE // 2
 N_BLOCK = 512
-WARM = 7
+WARM = 6
 QUADS = (0, 2, 1, 3)
+RUNS = (2, 4)
+RUN_OF = [(i, j) for i, n in enumerate(RUNS) for j in range(n)]
 W_CODES_AT, W_SCALES_AT, X_CODES_AT, X_SCALES_AT = 0, 64, 128, 192
 
 
@@ -51,11 +53,9 @@ def tile_deepseekv4attention_pb_kernel(tc, hidden_words, hidden_scales, wq_words
         def planes_at(name, passes, width, offset):
             return placed(name, passes * width, offset).rearrange("p (g n) -> p g n", g=passes)
 
-        xs_a0 = planes_at("xs_a0", 2, CHUNK, X_SCALES_AT)
-        xs_a1 = planes_at("xs_a1", PASSES - 2, CHUNK, X_SCALES_AT)
+        xs_a = [planes_at("xs_a%d" % i, n, CHUNK, X_SCALES_AT) for i, n in enumerate(RUNS)]
         xs_b = planes_at("xs_b", PASSES, 2 * CHUNK, X_SCALES_AT)
-        ws_a = planes_at("ws_a", 3, 1024, W_SCALES_AT)
-        ws_b = planes_at("ws_b", 3, 1024, W_SCALES_AT)
+        ws = [planes_at("ws%d" % i, n, 1024, W_SCALES_AT) for i, n in enumerate(RUNS)]
         x_a = [placed("x_a%d" % g, 2 * CHUNK, X_CODES_AT) for g in range(PASSES)]
         x_b = planes_at("x_b", PASSES, 2 * CHUNK, X_CODES_AT)
         x_c = planes_at("x_c", PASSES, 2 * CHUNK, X_CODES_AT)
@@ -64,21 +64,20 @@ def tile_deepseekv4attention_pb_kernel(tc, hidden_words, hidden_scales, wq_words
 
         nc.gpsimd.memset(warm[:], 0.0)
         nc.gpsimd.iota(pos[:], [[P, T_TILES]], base=0, channel_multiplier=1, allow_small_or_imprecise_dtypes=True)
-        for planes in (ws_a, xs_a0, xs_a1, ws_b, xs_b):
+        for planes in (ws[0], xs_a[0], xs_a[1], ws[1], xs_b):
             nc.vector.memset(planes.bitcast(I32), 0)
 
         load(x_a[0], hidden_words[0, :, 0 : 2 * CHUNK])
         load(w_0[0], wq_words[0, :, 0 : 2 * N_BLOCK])
-        load_scales(ws_a, wq_scales, 0, 3, 0, 1024)
-        load_scales(xs_a0, hidden_scales, 0, 2, 0, CHUNK)
+        load_scales(ws[0], wq_scales, 0, 2, 0, 1024)
+        load_scales(xs_a[0], hidden_scales, 0, 2, 0, CHUNK)
         load(w_0[1], wq_words[0, :, 2 * N_BLOCK : 4 * N_BLOCK])
         for g in range(1, PASSES):
             load(x_a[g], hidden_words[g, :, 0 : 2 * CHUNK])
             load(w_r[g - 1], wq_words[g, :, :])
             if g == 1:
-                load_scales(xs_a1, hidden_scales, 2, PASSES, 0, CHUNK)
-            if g == 2:
-                load_scales(ws_b, wq_scales, 3, PASSES, 0, 1024)
+                load_scales(xs_a[1], hidden_scales, 2, PASSES, 0, CHUNK)
+                load_scales(ws[1], wq_scales, 2, PASSES, 0, 1024)
         load_scales(xs_b, hidden_scales, 0, PASSES, CHUNK, 3 * CHUNK)
         load(x_b, hidden_words[:, :, 2 * CHUNK : 4 * CHUNK].rearrange("g p c -> p g c"))
         load(x_c, hidden_words[:, :, 4 * CHUNK : 6 * CHUNK].rearrange("g p c -> p g c"))
@@ -105,21 +104,21 @@ def tile_deepseekv4attention_pb_kernel(tc, hidden_words, hidden_scales, wq_words
 
         def x_operand(g, t):
             if t < 4:
-                scales = xs_a0[:, g] if g < 2 else xs_a1[:, g - 2]
-                return x_a[g][:, 256 * t : 256 * (t + 1)], scales[:, P * t : P * (t + 1)]
+                i, j = RUN_OF[g]
+                return x_a[g][:, 256 * t : 256 * (t + 1)], xs_a[i][:, j, P * t : P * (t + 1)]
             codes = x_b if t < 8 else x_c
             c = 256 * (t % 4)
             return codes[:, g, c : c + 256], xs_b[:, g, P * (t - 4) : P * (t - 3)]
 
         def w_operand(g, h0, nh):
             c0, c1 = HD * h0, HD * (h0 + nh)
-            planes = ws_a if g < 3 else ws_b
+            i, j = RUN_OF[g]
             if g == 0:
                 b = h0 // 4
                 codes = w_0[b][:, 2 * (c0 - N_BLOCK * b) : 2 * (c1 - N_BLOCK * b)]
             else:
                 codes = w_r[g - 1][:, 2 * c0 : 2 * c1]
-            return codes, planes[:, g % 3, c0:c1]
+            return codes, ws[i][:, j, c0:c1]
 
         def one_pass(acc, g, t, weights):
             xc, xs = x_operand(g, t)
@@ -130,13 +129,15 @@ def tile_deepseekv4attention_pb_kernel(tc, hidden_words, hidden_scales, wq_words
         def multiply(acc, t, nh):
             y = acc[:, 0 : HD * nh].rearrange("p (h d) -> p h d", d=HD)
             res = work.tile([P, nh, HD], F32, name="res")
-            if nh > 2:
-                nc.scalar.copy(out=res[:, :, 0 : HD - ROPE], in_=y[:, :, 0 : HD - ROPE])
             prod = work.tile([P, 2, nh, ROPE], F32, name="prod")
             shape = [P, 2, nh, ROPE]
-            nc.vector.tensor_tensor(out=prod[:], in0=y[:, :, HD - ROPE : HD].unsqueeze(1).to_broadcast(shape),
+            src = y
+            if t < T_TILES - 1:
+                nc.scalar.copy(out=res[:], in_=y)
+                src = res[:]
+            nc.vector.tensor_tensor(out=prod[:], in0=src[:, :, HD - ROPE : HD].unsqueeze(1).to_broadcast(shape),
                                     in1=table[:, t, :, :].unsqueeze(2).to_broadcast(shape), op=ALU.mult)
-            if nh <= 2:
+            if t == T_TILES - 1:
                 nc.scalar.copy(out=res[:, :, 0 : HD - ROPE], in_=y[:, :, 0 : HD - ROPE])
             return prod, res
 

import math
from contextlib import ExitStack

import concourse.mybir as mybir

FLOPS = 2 * 1536 * 1024 * 3072

F32 = mybir.dt.float32
BF16 = mybir.dt.bfloat16
I32 = mybir.dt.int32
U8 = mybir.dt.uint8
FP4X4 = mybir.dt.float4_e2m1fn_x4
ALU = mybir.AluOpType

P = 128
PASSES = 6
TOKENS = 1536
CHUNK = 512
T_TILES = TOKENS // P
HD = 128
ROPE = 64
HALF = ROPE // 2
N_BLOCK = 512
WARM = 6
QUADS = (0, 2, 1, 3)
RUNS = (2, 4)
RUN_OF = [(i, j) for i, n in enumerate(RUNS) for j in range(n)]
W_CODES_AT, W_SCALES_AT, X_CODES_AT, X_SCALES_AT = 0, 64, 128, 192


def tile_deepseekv4attention_pb_kernel(tc, hidden_words, hidden_scales, wq_words, wq_scales, out):
    nc = tc.nc
    with ExitStack() as ctx:
        keep = ctx.enter_context(tc.tile_pool(name="keep", bufs=1))
        work = ctx.enter_context(tc.tile_pool(name="work", bufs=6))
        psum = ctx.enter_context(tc.psum_pool(name="psum", bufs=8))
        ctx.enter_context(tc.manual_schedule())

        def load(tile_ap, dram_ap):
            nc.sync.dma_start(out=tile_ap.bitcast(I32), in_=dram_ap.bitcast(I32))

        def load_scales(planes, scales, g0, g1, c0, c1):
            for q in QUADS:
                load(planes[32 * q : 32 * q + 4, :, :],
                     scales[g0:g1, 4 * q : 4 * q + 4, c0:c1].rearrange("g r n -> r g n"))

        warm = keep.tile([P, 640], BF16, name="warm")
        pos = keep.tile([P, T_TILES], F32, name="pos")
        def placed(name, width, offset):
            whole_tile = keep.tile([P, offset + width], U8, name=name, align_bytes=256)
            return whole_tile[:, offset : offset + width]

        def planes_at(name, passes, width, offset):
            return placed(name, passes * width, offset).rearrange("p (g n) -> p g n", g=passes)

        xs_a = [planes_at("xs_a%d" % i, n, CHUNK, X_SCALES_AT) for i, n in enumerate(RUNS)]
        xs_b = planes_at("xs_b", PASSES, 2 * CHUNK, X_SCALES_AT)
        ws = [planes_at("ws%d" % i, n, 1024, W_SCALES_AT) for i, n in enumerate(RUNS)]
        x_a = [placed("x_a%d" % g, 2 * CHUNK, X_CODES_AT) for g in range(PASSES)]
        x_b = planes_at("x_b", PASSES, 2 * CHUNK, X_CODES_AT)
        x_c = planes_at("x_c", PASSES, 2 * CHUNK, X_CODES_AT)
        w_0 = [placed("w_0%d" % b, 2 * N_BLOCK, W_CODES_AT) for b in range(2)]
        w_r = [placed("w_r%d" % g, 4 * N_BLOCK, W_CODES_AT) for g in range(1, PASSES)]

        nc.gpsimd.memset(warm[:], 0.0)
        nc.gpsimd.iota(pos[:], [[P, T_TILES]], base=0, channel_multiplier=1, allow_small_or_imprecise_dtypes=True)
        for planes in (ws[0], xs_a[0], xs_a[1], ws[1], xs_b):
            nc.vector.memset(planes.bitcast(I32), 0)

        load(x_a[0], hidden_words[0, :, 0 : 2 * CHUNK])
        load(w_0[0], wq_words[0, :, 0 : 2 * N_BLOCK])
        load_scales(ws[0], wq_scales, 0, 2, 0, 1024)
        load_scales(xs_a[0], hidden_scales, 0, 2, 0, CHUNK)
        load(w_0[1], wq_words[0, :, 2 * N_BLOCK : 4 * N_BLOCK])
        for g in range(1, PASSES):
            load(x_a[g], hidden_words[g, :, 0 : 2 * CHUNK])
            load(w_r[g - 1], wq_words[g, :, :])
            if g == 1:
                load_scales(xs_a[1], hidden_scales, 2, PASSES, 0, CHUNK)
                load_scales(ws[1], wq_scales, 2, PASSES, 0, 1024)
        load_scales(xs_b, hidden_scales, 0, PASSES, CHUNK, 3 * CHUNK)
        load(x_b, hidden_words[:, :, 2 * CHUNK : 4 * CHUNK].rearrange("g p c -> p g c"))
        load(x_c, hidden_words[:, :, 4 * CHUNK : 6 * CHUNK].rearrange("g p c -> p g c"))

        ang = keep.tile([P, T_TILES, 2, ROPE], F32, name="ang")
        whole = keep.tile([P, T_TILES * 2 * ROPE], I32, name="whole")
        table = keep.tile([P, T_TILES, 2, ROPE], F32, name="table")
        turn = 1.0 / (2.0 * math.pi)
        pos3 = pos[:].unsqueeze(2)
        for kind, e, factor in ((0, 0, turn), (0, 1, turn), (1, 0, turn), (1, 1, -turn)):
            nc.vector.tensor_scalar(out=ang[:, :, kind, e : e + 1], in0=pos3, scalar1=factor, scalar2=None, op0=ALU.mult)
        rows = ang[:].rearrange("p t k c -> p (t k) c")
        s = 1
        while s < HALF:
            nc.vector.tensor_scalar(out=rows[:, :, 2 * s : 4 * s], in0=rows[:, :, 0 : 2 * s],
                                    scalar1=10000.0 ** (-s / HALF), scalar2=None, op0=ALU.mult)
            s *= 2
        nc.vector.tensor_scalar(out=ang[:, :, 0, :], in0=ang[:, :, 0, :], scalar1=0.25, scalar2=None, op0=ALU.add)
        flat = ang[:].rearrange("p t k c -> p (t k c)")
        nc.vector.tensor_copy(out=whole[:], in_=flat)
        nc.vector.tensor_tensor(out=flat, in0=flat, in1=whole[:], op=ALU.subtract)
        nc.scalar.activation(out=table[:].rearrange("p t k c -> p (t k c)"), in_=flat,
                             func=mybir.ActivationFunctionType.Sin, scale=2.0 * math.pi)

        def x_operand(g, t):
            if t < 4:
                i, j = RUN_OF[g]
                return x_a[g][:, 256 * t : 256 * (t + 1)], xs_a[i][:, j, P * t : P * (t + 1)]
            codes = x_b if t < 8 else x_c
            c = 256 * (t % 4)
            return codes[:, g, c : c + 256], xs_b[:, g, P * (t - 4) : P * (t - 3)]

        def w_operand(g, h0, nh):
            c0, c1 = HD * h0, HD * (h0 + nh)
            i, j = RUN_OF[g]
            if g == 0:
                b = h0 // 4
                codes = w_0[b][:, 2 * (c0 - N_BLOCK * b) : 2 * (c1 - N_BLOCK * b)]
            else:
                codes = w_r[g - 1][:, 2 * c0 : 2 * c1]
            return codes, ws[i][:, j, c0:c1]

        def one_pass(acc, g, t, weights):
            xc, xs = x_operand(g, t)
            wc, ws = weights
            nc.tensor.matmul_mx(out=acc[:, 0 : ws.shape[1]], lhsT=xc.bitcast(FP4X4), lhsT_scale=xs,
                                rhs=wc.bitcast(FP4X4), rhs_scale=ws, start=(g == 0), stop=(g == PASSES - 1))

        def multiply(acc, t, nh):
            y = acc[:, 0 : HD * nh].rearrange("p (h d) -> p h d", d=HD)
            res = work.tile([P, nh, HD], F32, name="res")
            prod = work.tile([P, 2, nh, ROPE], F32, name="prod")
            shape = [P, 2, nh, ROPE]
            src = y
            if t < T_TILES - 1:
                nc.scalar.copy(out=res[:], in_=y)
                src = res[:]
            nc.vector.tensor_tensor(out=prod[:], in0=src[:, :, HD - ROPE : HD].unsqueeze(1).to_broadcast(shape),
                                    in1=table[:, t, :, :].unsqueeze(2).to_broadcast(shape), op=ALU.mult)
            if t == T_TILES - 1:
                nc.scalar.copy(out=res[:, :, 0 : HD - ROPE], in_=y[:, :, 0 : HD - ROPE])
            return prod, res

        def add_and_store(prod, res, t, h0, nh):
            pair = "p h (j e) -> p h j e"
            nc.vector.tensor_tensor(out=res[:, :, HD - ROPE : HD].rearrange(pair, e=2),
                                    in0=prod[:, 0, :, :].rearrange(pair, e=2),
                                    in1=prod[:, 1, :, :].rearrange(pair, e=2)[:, :, :, ::-1], op=ALU.add)
            nc.sync.dma_start(out=out[0, h0 : h0 + nh, P * t : P * (t + 1), :].rearrange("h p d -> p h d"), in_=res[:])

        scrap = psum.tile([P, N_BLOCK], F32, name="acc")
        for k in range(WARM):
            nc.tensor.matmul(out=scrap[:], lhsT=warm[:, 0:P], rhs=warm[:, P : P + N_BLOCK], start=True, stop=True)

        first = [(t, 4 * b, psum.tile([P, N_BLOCK], F32, name="acc")) for b in range(2) for t in range(4)]
        for g in range(PASSES):
            for t, h0, acc in first:
                one_pass(acc, g, t, w_operand(g, h0, 4))
        def drain(groups):
            held = None
            for group in groups:
                acc, t, h0, nh = group
                parts = multiply(acc, t, nh)
                if held is not None:
                    add_and_store(*held)
                held = (*parts, t, h0, nh)
            add_and_store(*held)

        def compute(t, h0, nh):
            acc = psum.tile([P, N_BLOCK], F32, name="acc")
            for g in range(PASSES):
                one_pass(acc, g, t, w_operand(g, h0, nh))
            return acc, t, h0, nh

        drain([(acc, t, h0, 4) for t, h0, acc in first])
        for t in range(4, T_TILES - 1):
            for h0 in (0, 4):
                drain([compute(t, h0, 4)])
        last = T_TILES - 1
        drain([compute(last, 0, 4)])
        drain([compute(last, 4, 2), compute(last, 6, 1), compute(last, 7, 1)])
